import numpy as np
import ml_dtypes


def mxq(x, axis, fmt="e4m3"):
    dtype, down = {"e4m3": (ml_dtypes.float8_e4m3fn, 7), "e5m2": (ml_dtypes.float8_e5m2, 14)}[fmt]
    v = np.moveaxis(np.asarray(x, np.float32).astype(ml_dtypes.bfloat16).astype(np.float64), axis, -1)
    blocks = v.reshape(v.shape[:-1] + (-1, 32))
    amax = np.abs(blocks).max(-1, keepdims=True)
    byte = np.maximum(np.where(amax > 0, np.frexp(amax)[1] - 1 + 127, 0) - down, 1)
    scale = np.exp2(byte - 127.0)
    codes = (blocks / scale).astype(np.float32).astype(dtype).astype(np.float64)
    return np.moveaxis((codes * scale).reshape(v.shape), -1, axis)


WIDE = False


def mx_kscale(k):
    if not WIDE:
        return np.ones(k)
    levels = np.array([10, -10, 5, -5, 0])
    a = np.random.permutation(np.resize(levels, k // 512 * 4)).reshape(k // 512, 4)
    idx = np.arange(k)
    return np.exp2(a[idx // 512, idx % 128 // 32])


BF16 = ml_dtypes.bfloat16


def bf(x):
    return np.asarray(x, np.float32).astype(BF16)


def f64(x):
    return np.asarray(x).astype(np.float64)


E2M1 = np.array([0.0, 0.5, 1.0, 1.5, 2.0, 3.0, 4.0, 6.0, -0.0, -0.5, -1.0, -1.5, -2.0, -3.0, -4.0, -6.0])


def pack_weight(w, fmt):
    k, n = w.shape
    w = f64(bf(w)).reshape(k // 32, 32, n)
    amax = np.abs(w).max(1)
    if fmt == "e4m3":
        byte = np.frexp(amax)[1] - 1 + 127 - 7
    else:
        mant, ex = np.frexp(amax / 6.0)
        byte = np.where(mant > 0.5, ex, ex - 1) + 127
    byte = np.clip(np.where(amax > 0, byte, 1), 1, 254)
    scaled = (w * np.exp2(127.0 - byte)[:, None, :]).reshape(k, n).astype(np.float32)
    by_word = np.ascontiguousarray(scaled.reshape(k // 512, 128, 4, n).transpose(0, 1, 3, 2))
    if fmt == "e4m3":
        words = by_word.astype(ml_dtypes.float8_e4m3fn).view(np.uint8)
    else:
        c = by_word.astype(ml_dtypes.float4_e2m1fn).view(np.uint8) & 0xF
        words = c[..., 0::2] | (c[..., 1::2] << 4)
    return np.ascontiguousarray(words), np.ascontiguousarray(byte.astype(np.uint8).reshape(k // 512, 16, n))


def unpack_weight(words, scales, fmt):
    g, p, n, _ = words.shape
    if fmt == "e4m3":
        vals = np.ascontiguousarray(words).view(ml_dtypes.float8_e4m3fn).astype(np.float64)
    else:
        nib = np.empty((g, p, n, 4), np.uint8)
        nib[..., 0::2] = words & 0xF
        nib[..., 1::2] = words >> 4
        vals = E2M1[nib]
    vals = vals * np.repeat(np.exp2(scales.astype(np.float64) - 127.0), 8, axis=1)[..., None]
    return vals.transpose(0, 1, 3, 2).reshape(g * 512, n)

def pack4(w):
    words, scales = pack_weight(w, "e2m1")
    return words.reshape(words.shape[0], 128, -1), scales


def unpack4(words, scales):
    return unpack_weight(words.reshape(words.shape[0], 128, -1, 2), scales, "e2m1")


B, D = 2048, 1024


def setup_inputs():
    s = mx_kscale(D)
    x = bf(np.random.standard_normal((B, D)) * s)
    w = np.random.standard_normal((D, D)) * 0.04 / s[None, :]
    wm = np.tril(w, k=-1)
    words, scales = pack4(wm.T)
    b = bf(np.random.standard_normal(D) * 0.5)
    return {"x": x, "W_words": words, "W_scales": scales, "b": b}


def reference(x, W_words, W_scales, b):
    wt = unpack4(W_words, W_scales)
    return (mxq(f64(x), 1, "e4m3") @ wt) + f64(b)

@@ -1,0 +1,136 @@
+from contextlib import ExitStack
+
+import concourse.mybir as mybir
+from concourse.masks import make_identity
+
+F32 = mybir.dt.float32
+BF16 = mybir.dt.bfloat16
+I32 = mybir.dt.int32
+U32 = mybir.dt.uint32
+U8 = mybir.dt.uint8
+FP8X4 = mybir.dt.float8_e4m3fn_x4
+FP4X4 = mybir.dt.float4_e2m1fn_x4
+ADD = mybir.AluOpType.add
+
+P = 128
+B = 2048
+D = 1024
+TILES = B // P
+ROUNDS = TILES // 2
+FLOPS = 2 * B * D * D
+CHUNKS = [2, 2, 4, 4, 4]
+
+
+def tile_fvsbn_kernel(tc, x, W_words, W_scales, b, out):
+    nc = tc.nc
+    x_view = x.rearrange("(p t) d -> p t d", t=TILES)
+    out_view = out.rearrange("(p t) n -> p t n", t=TILES)
+    with ExitStack() as ctx:
+        keep = ctx.enter_context(tc.tile_pool(name="keep", bufs=1))
+        psum = ctx.enter_context(tc.psum_pool(name="psum", bufs=1))
+        ctx.enter_context(tc.manual_schedule())
+
+        w_planes = keep.tile([P, 2, D], U8, name="w_planes", align_bytes=64)
+        w_words = keep.tile([P, 2, 2 * D], U8, name="w_words", align_bytes=64)
+        b_rows = keep.tile([P, D], BF16, name="b_rows")
+        ones = keep.tile([P, P], BF16, name="ones")
+        ident = keep.tile([P, P], F32, name="ident")
+        bias = keep.tile([P, D], F32, name="bias")
+
+        nc.vector.memset(b_rows[:].bitcast(I32), 0)
+        nc.vector.memset(w_planes[:].rearrange("p g n -> p (g n)").bitcast(I32), 0)
+        nc.vector.memset(ones[:], 1.0)
+        make_identity(nc, ident[:])
+
+        nc.scalar.dma_start(out=b_rows[0:1, :], in_=b.rearrange("(o n) -> o n", o=1))
+
+        x_tiles = []
+
+        def load_x(c):
+            first = sum(CHUNKS[:c])
+            chunk = keep.tile([P, CHUNKS[c], D], BF16, name="x%d" % c)
+            nc.sync.dma_start(out=chunk[:], in_=x_view[:, first : first + CHUNKS[c], :])
+            for j in range(CHUNKS[c]):
+                x_tiles.append(chunk[:, j, :])
+
+        load_x(0)
+        scale_rows = W_scales.rearrange("g (q r) n -> r q g n", r=4)
+        for r in range(4):
+            nc.sync.dma_start(out=w_planes[r:P:32, :, :].bitcast(I32), in_=scale_rows[r].bitcast(I32))
+        nc.sync.dma_start(out=w_words[:, 0, :].bitcast(I32), in_=W_words[0].bitcast(I32))
+        load_x(1)
+        nc.sync.dma_start(out=w_words[:, 1, D : 2 * D].bitcast(I32), in_=W_words[1][:, D : 2 * D].bitcast(I32))
+        for c in range(2, len(CHUNKS)):
+            load_x(c)
+
+        grouped = {}
+        codes = {}
+        planes = {}
+
+        def transposes(r):
+            grouped[r] = keep.tile([P, 2, D], BF16, name="grouped%d" % r, align_bytes=64)
+            for i in range(2):
+                words = x_tiles[2 * r + i].bitcast(F32)
+                xt = psum.tile([P, 4, P], F32, name="xt", tag="xt", bufs=2)
+                for g in range(2):
+                    for u in range(2):
+                        nc.tensor.transpose(xt[:, 2 * g + u, :], words[:, 256 * g + u : 256 * (g + 1) : 2], ident[:])
+                nc.scalar.copy(
+                    out=grouped[r][:, i, :].bitcast(F32).rearrange("p (g r u) -> p g r u", g=2, u=2),
+                    in_=xt[:].rearrange("p (g u) r -> p g r u", g=2),
+                )
+
+        def quantise(r):
+            codes[r] = keep.tile([P, 4 * P], U32, name="codes%d" % r, align_bytes=64)
+            planes[r] = keep.tile([P, 4 * P], U8, name="planes%d" % r, align_bytes=64)
+            nc.vector.quantize_mx(
+                out=codes[r][:].bitcast(FP8X4),
+                scales=planes[r][:],
+                in_=grouped[r][:].rearrange("p i d -> p (i d)"),
+            )
+
+        def mx_pass(acc, r, i, g, h, start, stop):
+            cols = slice(256 * i + P * g, 256 * i + P * (g + 1))
+            nc.tensor.matmul_mx(
+                out=acc[:],
+                lhsT=codes[r][:, cols].bitcast(FP8X4),
+                lhsT_scale=planes[r][:, cols],
+                rhs=w_words[:, g, D * h : D * (h + 1)].bitcast(FP4X4),
+                rhs_scale=w_planes[:, g, 512 * h : 512 * (h + 1)],
+                start=start,
+                stop=stop,
+            )
+
+        def multiply(r):
+            accs = []
+            for i in range(2):
+                low = psum.tile([P, 512], F32, name="acc", tag="acc", bufs=6)
+                mx_pass(low, r, i, 0, 0, True, True)
+                high = psum.tile([P, 512], F32, name="acc", tag="acc", bufs=6)
+                mx_pass(high, r, i, 0, 1, True, False)
+                mx_pass(high, r, i, 1, 1, False, True)
+                accs.append((low, high))
+            return accs
+
+        def finish(r, accs):
+            result = keep.tile([P, 2, D], F32, name="result%d" % r)
+            for i in range(2):
+                for h in range(2):
+                    half = slice(512 * h, 512 * (h + 1))
+                    nc.vector.tensor_tensor(out=result[:, i, half], in0=accs[i][h][:], in1=bias[:, half], op=ADD)
+            nc.sync.dma_start(out=out_view[:, 2 * r : 2 * r + 2, :], in_=result[:])
+
+        transposes(0)
+        for h in range(2):
+            spread = psum.tile([P, 512], F32, name="acc", tag="acc", bufs=6)
+            nc.tensor.matmul(out=spread[:], lhsT=ones[:], rhs=b_rows[:, 512 * h : 512 * (h + 1)], start=True, stop=True)
+            nc.scalar.copy(out=bias[:, 512 * h : 512 * (h + 1)], in_=spread[:])
+        quantise(0)
+        transposes(1)
+        for r in range(ROUNDS):
+            accs = multiply(r)
+            if r + 2 < ROUNDS:
+                transposes(r + 2)
+            if r + 1 < ROUNDS:
+                quantise(r + 1)
+            finish(r, accs)

@@ -18,7 +18,8 @@ D = 1024
 TILES = B // P
 ROUNDS = TILES // 2
 FLOPS = 2 * B * D * D
-CHUNKS = [2, 2, 4, 4, 4]
+CHUNKS = [1, 1, 2, 4, 4, 4]
+OFFLOAD = True
 
 
 def tile_fvsbn_kernel(tc, x, W_words, W_scales, b, out):
@@ -63,74 +64,99 @@ def tile_fvsbn_kernel(tc, x, W_words, W_scales, b, out):
         for c in range(2, len(CHUNKS)):
             load_x(c)
 
-        grouped = {}
-        codes = {}
-        planes = {}
+        grouped = [keep.tile([P, 2, D], BF16, name="grouped%d" % r, align_bytes=64) for r in range(ROUNDS)]
+        codes = [keep.tile([P, 4 * P], U32, name="codes%d" % r, align_bytes=64) for r in range(ROUNDS)]
+        planes = [keep.tile([P, 4 * P], U8, name="planes%d" % r, align_bytes=64) for r in range(ROUNDS)]
+        result = [keep.tile([P, 2, D], F32, name="result%d" % r) for r in range(ROUNDS)]
 
-        def transposes(r):
-            grouped[r] = keep.tile([P, 2, D], BF16, name="grouped%d" % r, align_bytes=64)
-            for i in range(2):
-                words = x_tiles[2 * r + i].bitcast(F32)
-                xt = psum.tile([P, 4, P], F32, name="xt", tag="xt", bufs=2)
-                for g in range(2):
-                    for u in range(2):
-                        nc.tensor.transpose(xt[:, 2 * g + u, :], words[:, 256 * g + u : 256 * (g + 1) : 2], ident[:])
-                nc.scalar.copy(
-                    out=grouped[r][:, i, :].bitcast(F32).rearrange("p (g r u) -> p g r u", g=2, u=2),
-                    in_=xt[:].rearrange("p (g u) r -> p g r u", g=2),
-                )
-
-        def quantise(r):
-            codes[r] = keep.tile([P, 4 * P], U32, name="codes%d" % r, align_bytes=64)
-            planes[r] = keep.tile([P, 4 * P], U8, name="planes%d" % r, align_bytes=64)
-            nc.vector.quantize_mx(
-                out=codes[r][:].bitcast(FP8X4),
-                scales=planes[r][:],
-                in_=grouped[r][:].rearrange("p i d -> p (i d)"),
+        def transposes(t):
+            words = x_tiles[t].bitcast(F32)
+            xt = psum.tile([P, 4, P], F32, name="xt", tag="xt", bufs=2)
+            for g in range(2):
+                for u in range(2):
+                    nc.tensor.transpose(xt[:, 2 * g + u, :], words[:, 256 * g + u : 256 * (g + 1) : 2], ident[:])
+            nc.scalar.copy(
+                out=grouped[t // 2][:, t % 2, :].bitcast(F32).rearrange("p (g r u) -> p g r u", g=2, u=2),
+                in_=xt[:].rearrange("p (g u) r -> p g r u", g=2),
             )
 
-        def mx_pass(acc, r, i, g, h, start, stop):
-            cols = slice(256 * i + P * g, 256 * i + P * (g + 1))
+        def quantise(r, first, count):
+            nc.vector.quantize_mx(
+                out=codes[r][:, 256 * first : 256 * (first + count)].bitcast(FP8X4),
+                scales=planes[r][:, 256 * first : 256 * (first + count)],
+                in_=grouped[r][:, first : first + count, :].rearrange("p i d -> p (i d)"),
+            )
+
+        def mx_pass(acc, t, g, h, start, stop):
+            cols = slice(256 * (t % 2) + P * g, 256 * (t % 2) + P * (g + 1))
             nc.tensor.matmul_mx(
                 out=acc[:],
-                lhsT=codes[r][:, cols].bitcast(FP8X4),
-                lhsT_scale=planes[r][:, cols],
+                lhsT=codes[t // 2][:, cols].bitcast(FP8X4),
+                lhsT_scale=planes[t // 2][:, cols],
                 rhs=w_words[:, g, D * h : D * (h + 1)].bitcast(FP4X4),
                 rhs_scale=w_planes[:, g, 512 * h : 512 * (h + 1)],
                 start=start,
                 stop=stop,
             )
 
-        def multiply(r):
-            accs = []
-            for i in range(2):
-                low = psum.tile([P, 512], F32, name="acc", tag="acc", bufs=6)
-                mx_pass(low, r, i, 0, 0, True, True)
-                high = psum.tile([P, 512], F32, name="acc", tag="acc", bufs=6)
-                mx_pass(high, r, i, 0, 1, True, False)
-                mx_pass(high, r, i, 1, 1, False, True)
-                accs.append((low, high))
-            return accs
+        def multiply(t):
+            low = psum.tile([P, 512], F32, name="acc", tag="acc", bufs=6)
+            mx_pass(low, t, 0, 0, True, True)
+            if OFFLOAD and t % 2 == 0:
+                nc.scalar.copy(out=result[t // 2][:, 0, 0:512], in_=low[:])
+            high = psum.tile([P, 512], F32, name="acc", tag="acc", bufs=6)
+            mx_pass(high, t, 0, 1, True, False)
+            mx_pass(high, t, 1, 1, False, True)
+            return (low, high)
 
-        def finish(r, accs):
-            result = keep.tile([P, 2, D], F32, name="result%d" % r)
-            for i in range(2):
-                for h in range(2):
-                    half = slice(512 * h, 512 * (h + 1))
-                    nc.vector.tensor_tensor(out=result[:, i, half], in0=accs[i][h][:], in1=bias[:, half], op=ADD)
-            nc.sync.dma_start(out=out_view[:, 2 * r : 2 * r + 2, :], in_=result[:])
+        def add_bias(t, h, accs):
+            half = slice(512 * h, 512 * (h + 1))
+            dst = result[t // 2][:, t % 2, half]
+            if OFFLOAD and t % 2 == 0 and h == 0:
+                nc.gpsimd.tensor_tensor(out=dst, in0=dst, in1=bias[:, half], op=ADD)
+            else:
+                nc.vector.tensor_tensor(out=dst, in0=accs[h][:], in1=bias[:, half], op=ADD)
 
         transposes(0)
         for h in range(2):
             spread = psum.tile([P, 512], F32, name="acc", tag="acc", bufs=6)
             nc.tensor.matmul(out=spread[:], lhsT=ones[:], rhs=b_rows[:, 512 * h : 512 * (h + 1)], start=True, stop=True)
             nc.scalar.copy(out=bias[:, 512 * h : 512 * (h + 1)], in_=spread[:])
-        quantise(0)
+        quantise(0, 0, 1)
         transposes(1)
-        for r in range(ROUNDS):
-            accs = multiply(r)
+        quantise(0, 1, 1)
+        acc_a = multiply(0)
+        transposes(2)
+        transposes(3)
+        acc_b = multiply(1)
+        transposes(4)
+        transposes(5)
+        add_bias(0, 0, acc_a)
+        add_bias(0, 1, acc_a)
+        add_bias(1, 0, acc_b)
+        quantise(1, 0, 2)
+        add_bias(1, 1, acc_b)
+        nc.sync.dma_start(out=out_view[:, 0:2, :], in_=result[0][:])
+
+        for r in range(1, ROUNDS):
+            acc_a = multiply(2 * r)
+            acc_b = multiply(2 * r + 1)
             if r + 2 < ROUNDS:
-                transposes(r + 2)
+                transposes(2 * r + 4)
+                transposes(2 * r + 5)
             if r + 1 < ROUNDS:
-                quantise(r + 1)
-            finish(r, accs)
+                quantise(r + 1, 0, 2)
+            add_bias(2 * r, 0, acc_a)
+            add_bias(2 * r, 1, acc_a)
+            if r == ROUNDS - 1:
+                nc.sync.dma_start(out=out_view[:, 2 * r, :], in_=result[r][:, 0, :])
+                for h in range(2):
+                    add_bias(2 * r + 1, h, acc_b)
+                    nc.sync.dma_start(
+                        out=out_view[:, 2 * r + 1, 512 * h : 512 * (h + 1)],
+                        in_=result[r][:, 1, 512 * h : 512 * (h + 1)],
+                    )
+            else:
+                add_bias(2 * r + 1, 0, acc_b)
+                add_bias(2 * r + 1, 1, acc_b)
+                nc.sync.dma_start(out=out_view[:, 2 * r : 2 * r + 2, :], in_=result[r][:])

@@ -18,8 +18,11 @@ D = 1024
 TILES = B // P
 ROUNDS = TILES // 2
 FLOPS = 2 * B * D * D
-CHUNKS = [1, 1, 2, 4, 4, 4]
-OFFLOAD = True
+CHUNKS = [1,1,2,4,4,4]
+OFFLOAD_ROUNDS = 8
+FINE_FROM = 4
+HALVES_FROM = 6
+SORTED = [5,7,9,11,13,15]
 
 
 def tile_fvsbn_kernel(tc, x, W_words, W_scales, b, out):
@@ -68,13 +71,25 @@ def tile_fvsbn_kernel(tc, x, W_words, W_scales, b, out):
         codes = [keep.tile([P, 4 * P], U32, name="codes%d" % r, align_bytes=64) for r in range(ROUNDS)]
         planes = [keep.tile([P, 4 * P], U8, name="planes%d" % r, align_bytes=64) for r in range(ROUNDS)]
         result = [keep.tile([P, 2, D], F32, name="result%d" % r) for r in range(ROUNDS)]
+        sorted_words = {}
+
+        def sort_words(t):
+            if t in SORTED:
+                sorted_words[t] = keep.tile([P, 4, P], F32, name="sorted%d" % t)
+                nc.scalar.copy(
+                    out=sorted_words[t][:].rearrange("p (g u) j -> p g u j", g=2),
+                    in_=x_tiles[t].bitcast(F32).rearrange("p (g j u) -> p g u j", g=2, u=2),
+                )
 
         def transposes(t):
             words = x_tiles[t].bitcast(F32)
             xt = psum.tile([P, 4, P], F32, name="xt", tag="xt", bufs=2)
             for g in range(2):
                 for u in range(2):
-                    nc.tensor.transpose(xt[:, 2 * g + u, :], words[:, 256 * g + u : 256 * (g + 1) : 2], ident[:])
+                    if t in SORTED:
+                        nc.tensor.transpose(xt[:, 2 * g + u, :], sorted_words[t][:, 2 * g + u, :], ident[:])
+                    else:
+                        nc.tensor.transpose(xt[:, 2 * g + u, :], words[:, 256 * g + u : 256 * (g + 1) : 2], ident[:])
             nc.scalar.copy(
                 out=grouped[t // 2][:, t % 2, :].bitcast(F32).rearrange("p (g r u) -> p g r u", g=2, u=2),
                 in_=xt[:].rearrange("p (g u) r -> p g r u", g=2),
@@ -99,10 +114,13 @@ def tile_fvsbn_kernel(tc, x, W_words, W_scales, b, out):
                 stop=stop,
             )
 
+        def offloaded(t):
+            return t % 2 == 0 and t // 2 < OFFLOAD_ROUNDS
+
         def multiply(t):
             low = psum.tile([P, 512], F32, name="acc", tag="acc", bufs=6)
             mx_pass(low, t, 0, 0, True, True)
-            if OFFLOAD and t % 2 == 0:
+            if offloaded(t):
                 nc.scalar.copy(out=result[t // 2][:, 0, 0:512], in_=low[:])
             high = psum.tile([P, 512], F32, name="acc", tag="acc", bufs=6)
             mx_pass(high, t, 0, 1, True, False)
@@ -112,10 +130,13 @@ def tile_fvsbn_kernel(tc, x, W_words, W_scales, b, out):
         def add_bias(t, h, accs):
             half = slice(512 * h, 512 * (h + 1))
             dst = result[t // 2][:, t % 2, half]
-            if OFFLOAD and t % 2 == 0 and h == 0:
+            if offloaded(t) and h == 0:
                 nc.gpsimd.tensor_tensor(out=dst, in0=dst, in1=bias[:, half], op=ADD)
             else:
                 nc.vector.tensor_tensor(out=dst, in0=accs[h][:], in1=bias[:, half], op=ADD)
+
+        def store(t, cols):
+            nc.sync.dma_start(out=out_view[:, t, cols], in_=result[t // 2][:, t % 2, cols])
 
         transposes(0)
         for h in range(2):
@@ -125,9 +146,13 @@ def tile_fvsbn_kernel(tc, x, W_words, W_scales, b, out):
         quantise(0, 0, 1)
         transposes(1)
         quantise(0, 1, 1)
+        sort_words(2)
+        sort_words(3)
         acc_a = multiply(0)
         transposes(2)
         transposes(3)
+        sort_words(4)
+        sort_words(5)
         acc_b = multiply(1)
         transposes(4)
         transposes(5)
@@ -140,23 +165,36 @@ def tile_fvsbn_kernel(tc, x, W_words, W_scales, b, out):
 
         for r in range(1, ROUNDS):
             acc_a = multiply(2 * r)
+            if r + 2 < ROUNDS:
+                sort_words(2 * r + 4)
+                sort_words(2 * r + 5)
             acc_b = multiply(2 * r + 1)
             if r + 2 < ROUNDS:
                 transposes(2 * r + 4)
                 transposes(2 * r + 5)
             if r + 1 < ROUNDS:
                 quantise(r + 1, 0, 2)
-            add_bias(2 * r, 0, acc_a)
-            add_bias(2 * r, 1, acc_a)
-            if r == ROUNDS - 1:
-                nc.sync.dma_start(out=out_view[:, 2 * r, :], in_=result[r][:, 0, :])
-                for h in range(2):
-                    add_bias(2 * r + 1, h, acc_b)
-                    nc.sync.dma_start(
-                        out=out_view[:, 2 * r + 1, 512 * h : 512 * (h + 1)],
-                        in_=result[r][:, 1, 512 * h : 512 * (h + 1)],
-                    )
+            low_half = slice(0, 512)
+            high_half = slice(512, D)
+            if r >= HALVES_FROM:
+                add_bias(2 * r, 1, acc_a)
+                store(2 * r, high_half)
+                add_bias(2 * r, 0, acc_a)
+                store(2 * r, low_half)
+                add_bias(2 * r + 1, 0, acc_b)
+                store(2 * r + 1, low_half)
+                add_bias(2 * r + 1, 1, acc_b)
+                store(2 * r + 1, high_half)
+            elif r >= FINE_FROM:
+                add_bias(2 * r, 0, acc_a)
+                add_bias(2 * r, 1, acc_a)
+                store(2 * r, slice(0, D))
+                add_bias(2 * r + 1, 0, acc_b)
+                add_bias(2 * r + 1, 1, acc_b)
+                store(2 * r + 1, slice(0, D))
             else:
+                add_bias(2 * r, 0, acc_a)
+                add_bias(2 * r, 1, acc_a)
                 add_bias(2 * r + 1, 0, acc_b)
                 add_bias(2 * r + 1, 1, acc_b)
                 nc.sync.dma_start(out=out_view[:, 2 * r : 2 * r + 2, :], in_=result[r][:])

@@ -22,7 +22,7 @@ CHUNKS = [1,1,2,4,4,4]
 OFFLOAD_ROUNDS = 8
 FINE_FROM = 4
 HALVES_FROM = 6
-SORTED = [5,7,9,11,13,15]
+SORTED = []
 
 
 def tile_fvsbn_kernel(tc, x, W_words, W_scales, b, out):

@@ -22,7 +22,7 @@ CHUNKS = [1,1,2,4,4,4]
 OFFLOAD_ROUNDS = 8
 FINE_FROM = 4
 HALVES_FROM = 6
-SORTED = []
+SORTED = [7,9,11,13,15]
 
 
 def tile_fvsbn_kernel(tc, x, W_words, W_scales, b, out):
@@ -164,10 +164,10 @@ def tile_fvsbn_kernel(tc, x, W_words, W_scales, b, out):
         nc.sync.dma_start(out=out_view[:, 0:2, :], in_=result[0][:])
 
         for r in range(1, ROUNDS):
-            acc_a = multiply(2 * r)
             if r + 2 < ROUNDS:
                 sort_words(2 * r + 4)
                 sort_words(2 * r + 5)
+            acc_a = multiply(2 * r)
             acc_b = multiply(2 * r + 1)
             if r + 2 < ROUNDS:
                 transposes(2 * r + 4)

from contextlib import ExitStack

import concourse.mybir as mybir
from concourse.masks import make_identity

F32 = mybir.dt.float32
BF16 = mybir.dt.bfloat16
I32 = mybir.dt.int32
U32 = mybir.dt.uint32
U8 = mybir.dt.uint8
FP8X4 = mybir.dt.float8_e4m3fn_x4
FP4X4 = mybir.dt.float4_e2m1fn_x4
ADD = mybir.AluOpType.add

P = 128
B = 2048
D = 1024
TILES = B // P
ROUNDS = TILES // 2
FLOPS = 2 * B * D * D
CHUNKS = [1,1,2,4,4,4]
OFFLOAD_ROUNDS = 8
FINE_FROM = 4
HALVES_FROM = 6
SORTED = [7,9,11,13,15]


def tile_fvsbn_kernel(tc, x, W_words, W_scales, b, out):
    nc = tc.nc
    x_view = x.rearrange("(p t) d -> p t d", t=TILES)
    out_view = out.rearrange("(p t) n -> p t n", t=TILES)
    with ExitStack() as ctx:
        keep = ctx.enter_context(tc.tile_pool(name="keep", bufs=1))
        psum = ctx.enter_context(tc.psum_pool(name="psum", bufs=1))
        ctx.enter_context(tc.manual_schedule())

        w_planes = keep.tile([P, 2, D], U8, name="w_planes", align_bytes=64)
        w_words = keep.tile([P, 2, 2 * D], U8, name="w_words", align_bytes=64)
        b_rows = keep.tile([P, D], BF16, name="b_rows")
        ones = keep.tile([P, P], BF16, name="ones")
        ident = keep.tile([P, P], F32, name="ident")
        bias = keep.tile([P, D], F32, name="bias")

        nc.vector.memset(b_rows[:].bitcast(I32), 0)
        nc.vector.memset(w_planes[:].rearrange("p g n -> p (g n)").bitcast(I32), 0)
        nc.vector.memset(ones[:], 1.0)
        make_identity(nc, ident[:])

        nc.scalar.dma_start(out=b_rows[0:1, :], in_=b.rearrange("(o n) -> o n", o=1))

        x_tiles = []

        def load_x(c):
            first = sum(CHUNKS[:c])
            chunk = keep.tile([P, CHUNKS[c], D], BF16, name="x%d" % c)
            nc.sync.dma_start(out=chunk[:], in_=x_view[:, first : first + CHUNKS[c], :])
            for j in range(CHUNKS[c]):
                x_tiles.append(chunk[:, j, :])

        load_x(0)
        scale_rows = W_scales.rearrange("g (q r) n -> r q g n", r=4)
        for r in range(4):
            nc.sync.dma_start(out=w_planes[r:P:32, :, :].bitcast(I32), in_=scale_rows[r].bitcast(I32))
        nc.sync.dma_start(out=w_words[:, 0, :].bitcast(I32), in_=W_words[0].bitcast(I32))
        load_x(1)
        nc.sync.dma_start(out=w_words[:, 1, D : 2 * D].bitcast(I32), in_=W_words[1][:, D : 2 * D].bitcast(I32))
        for c in range(2, len(CHUNKS)):
            load_x(c)

        grouped = [keep.tile([P, 2, D], BF16, name="grouped%d" % r, align_bytes=64) for r in range(ROUNDS)]
        codes = [keep.tile([P, 4 * P], U32, name="codes%d" % r, align_bytes=64) for r in range(ROUNDS)]
        planes = [keep.tile([P, 4 * P], U8, name="planes%d" % r, align_bytes=64) for r in range(ROUNDS)]
        result = [keep.tile([P, 2, D], F32, name="result%d" % r) for r in range(ROUNDS)]
        sorted_words = {}

        def sort_words(t):
            if t in SORTED:
                sorted_words[t] = keep.tile([P, 4, P], F32, name="sorted%d" % t)
                nc.scalar.copy(
                    out=sorted_words[t][:].rearrange("p (g u) j -> p g u j", g=2),
                    in_=x_tiles[t].bitcast(F32).rearrange("p (g j u) -> p g u j", g=2, u=2),
                )

        def transposes(t):
            words = x_tiles[t].bitcast(F32)
            xt = psum.tile([P, 4, P], F32, name="xt", tag="xt", bufs=2)
            for g in range(2):
                for u in range(2):
                    if t in SORTED:
                        nc.tensor.transpose(xt[:, 2 * g + u, :], sorted_words[t][:, 2 * g + u, :], ident[:])
                    else:
                        nc.tensor.transpose(xt[:, 2 * g + u, :], words[:, 256 * g + u : 256 * (g + 1) : 2], ident[:])
            nc.scalar.copy(
                out=grouped[t // 2][:, t % 2, :].bitcast(F32).rearrange("p (g r u) -> p g r u", g=2, u=2),
                in_=xt[:].rearrange("p (g u) r -> p g r u", g=2),
            )

        def quantise(r, first, count):
            nc.vector.quantize_mx(
                out=codes[r][:, 256 * first : 256 * (first + count)].bitcast(FP8X4),
                scales=planes[r][:, 256 * first : 256 * (first + count)],
                in_=grouped[r][:, first : first + count, :].rearrange("p i d -> p (i d)"),
            )

        def mx_pass(acc, t, g, h, start, stop):
            cols = slice(256 * (t % 2) + P * g, 256 * (t % 2) + P * (g + 1))
            nc.tensor.matmul_mx(
                out=acc[:],
                lhsT=codes[t // 2][:, cols].bitcast(FP8X4),
                lhsT_scale=planes[t // 2][:, cols],
                rhs=w_words[:, g, D * h : D * (h + 1)].bitcast(FP4X4),
                rhs_scale=w_planes[:, g, 512 * h : 512 * (h + 1)],
                start=start,
                stop=stop,
            )

        def offloaded(t):
            return t % 2 == 0 and t // 2 < OFFLOAD_ROUNDS

        def multiply(t):
            low = psum.tile([P, 512], F32, name="acc", tag="acc", bufs=6)
            mx_pass(low, t, 0, 0, True, True)
            if offloaded(t):
                nc.scalar.copy(out=result[t // 2][:, 0, 0:512], in_=low[:])
            high = psum.tile([P, 512], F32, name="acc", tag="acc", bufs=6)
            mx_pass(high, t, 0, 1, True, False)
            mx_pass(high, t, 1, 1, False, True)
            return (low, high)

        def add_bias(t, h, accs):
            half = slice(512 * h, 512 * (h + 1))
            dst = result[t // 2][:, t % 2, half]
            if offloaded(t) and h == 0:
                nc.gpsimd.tensor_tensor(out=dst, in0=dst, in1=bias[:, half], op=ADD)
            else:
                nc.vector.tensor_tensor(out=dst, in0=accs[h][:], in1=bias[:, half], op=ADD)

        def store(t, cols):
            nc.sync.dma_start(out=out_view[:, t, cols], in_=result[t // 2][:, t % 2, cols])

        transposes(0)
        for h in range(2):
            spread = psum.tile([P, 512], F32, name="acc", tag="acc", bufs=6)
            nc.tensor.matmul(out=spread[:], lhsT=ones[:], rhs=b_rows[:, 512 * h : 512 * (h + 1)], start=True, stop=True)
            nc.scalar.copy(out=bias[:, 512 * h : 512 * (h + 1)], in_=spread[:])
        quantise(0, 0, 1)
        transposes(1)
        quantise(0, 1, 1)
        sort_words(2)
        sort_words(3)
        acc_a = multiply(0)
        transposes(2)
        transposes(3)
        sort_words(4)
        sort_words(5)
        acc_b = multiply(1)
        transposes(4)
        transposes(5)
        add_bias(0, 0, acc_a)
        add_bias(0, 1, acc_a)
        add_bias(1, 0, acc_b)
        quantise(1, 0, 2)
        add_bias(1, 1, acc_b)
        nc.sync.dma_start(out=out_view[:, 0:2, :], in_=result[0][:])

        for r in range(1, ROUNDS):
            if r + 2 < ROUNDS:
                sort_words(2 * r + 4)
                sort_words(2 * r + 5)
            acc_a = multiply(2 * r)
            acc_b = multiply(2 * r + 1)
            if r + 2 < ROUNDS:
                transposes(2 * r + 4)
                transposes(2 * r + 5)
            if r + 1 < ROUNDS:
                quantise(r + 1, 0, 2)
            low_half = slice(0, 512)
            high_half = slice(512, D)
            if r >= HALVES_FROM:
                add_bias(2 * r, 1, acc_a)
                store(2 * r, high_half)
                add_bias(2 * r, 0, acc_a)
                store(2 * r, low_half)
                add_bias(2 * r + 1, 0, acc_b)
                store(2 * r + 1, low_half)
                add_bias(2 * r + 1, 1, acc_b)
                store(2 * r + 1, high_half)
            elif r >= FINE_FROM:
                add_bias(2 * r, 0, acc_a)
                add_bias(2 * r, 1, acc_a)
                store(2 * r, slice(0, D))
                add_bias(2 * r + 1, 0, acc_b)
                add_bias(2 * r + 1, 1, acc_b)
                store(2 * r + 1, slice(0, D))
            else:
                add_bias(2 * r, 0, acc_a)
                add_bias(2 * r, 1, acc_a)
                add_bias(2 * r + 1, 0, acc_b)
                add_bias(2 * r + 1, 1, acc_b)
                nc.sync.dma_start(out=out_view[:, 2 * r : 2 * r + 2, :], in_=result[r][:])
